import numpy as np
import ml_dtypes

BF16 = ml_dtypes.bfloat16


def bf(x):
    return np.asarray(x, np.float32).astype(BF16)


def f32(x):
    return np.asarray(x, np.float32)


def f64(x):
    return np.asarray(x).astype(np.float64)


def striped(idx):
    return np.tile(idx.reshape(-1, 16).T, (8, 1))


H, M, CH, ROT, S, N = 256, 256, 128, 32, 2048, 1024
THETA = 10000.0


def rope_table():
    inv_freq = 1.0 / THETA ** (np.arange(0, ROT, 2) / ROT)
    ang = np.einsum("i,j->ij", np.arange(S), inv_freq).astype(np.float32)
    pair = (np.arange(CH) % ROT) // 2
    return np.concatenate([np.cos(ang).T[pair], np.sin(ang).T[pair]], axis=0)


def setup_inputs():
    return {"tab": f32(rope_table()), "h": bf(np.random.standard_normal((H, N))), "w": bf(np.random.standard_normal((H, M)) / np.sqrt(H)), "offs": striped(np.random.permutation(np.tile(np.arange(S), 2))[:N])}


def reference(tab, h, w, offs):
    idx = offs[:16].T.reshape(-1)
    t = f64(w).T @ f64(h)
    r = np.empty_like(t)
    r[0::2] = -t[1::2]
    r[1::2] = t[0::2]
    cos = np.tile(f64(tab)[:CH][:, idx], (M // CH, 1))
    sin = np.tile(f64(tab)[CH:][:, idx], (M // CH, 1))
    return cos * t + sin * r

@@ -1,0 +1,65 @@
+import concourse.mybir as mybir
+
+P = 128
+H, M, S, N = 256, 256, 2048, 1024
+KB = H // P
+CB = M // P
+PIECE = 512
+FLOPS = 2 * H * M * N
+
+BF16, F32, U16 = mybir.dt.bfloat16, mybir.dt.float32, mybir.dt.uint16
+MULT, ADD = mybir.AluOpType.mult, mybir.AluOpType.add
+
+
+def tile_codegenattention_kernel(tc, tab, h, w, offs, out):
+    nc = tc.nc
+    with (
+        tc.tile_pool(name="held", bufs=1) as held,
+        tc.tile_pool(name="work", bufs=2) as work,
+        tc.psum_pool(name="psum", bufs=2) as psum,
+    ):
+        offsets = held.tile([P, N // 16], U16, name="offsets")
+        nc.sync.dma_start(offsets[:], offs)
+        w_sb = held.tile([P, KB, M], BF16, name="w_sb")
+        nc.sync.dma_start(w_sb[:], w.rearrange("(kb p) c -> p kb c", p=P))
+        h_sb = held.tile([P, KB, N], BF16, name="h_sb")
+        nc.sync.dma_start(h_sb[:], h.rearrange("(kb p) j -> p kb j", p=P))
+        cos = held.tile([P, S], F32, name="cos")
+        nc.scalar.dma_start(cos[:], tab[0:P, :])
+        sin = held.tile([P, S], F32, name="sin")
+        nc.scalar.dma_start(sin[:], tab[P : 2 * P, :])
+
+        w_rot = held.tile([P, KB, M], BF16, name="w_rot")
+        w_pairs = w_sb[:].rearrange("p kb (i two) -> p kb i two", two=2)
+        rot_pairs = w_rot[:].rearrange("p kb (i two) -> p kb i two", two=2)
+        nc.vector.tensor_scalar_mul(rot_pairs[:, :, :, 0:1], w_pairs[:, :, :, 1:2], -1.0)
+        nc.vector.tensor_copy(rot_pairs[:, :, :, 1:2], w_pairs[:, :, :, 0:1])
+
+        for cb in range(CB):
+            channels = slice(cb * P, (cb + 1) * P)
+            for piece in range(N // PIECE):
+                tokens = slice(piece * PIECE, (piece + 1) * PIECE)
+                picked = offsets[:, piece * (PIECE // 16) : (piece + 1) * (PIECE // 16)]
+
+                t_ps = psum.tile([P, PIECE], F32, name="t_ps")
+                r_ps = psum.tile([P, PIECE], F32, name="r_ps")
+                for kb in range(KB):
+                    nc.tensor.matmul(
+                        t_ps[:], w_sb[:, kb, channels], h_sb[:, kb, tokens], start=kb == 0, stop=kb == KB - 1
+                    )
+                for kb in range(KB):
+                    nc.tensor.matmul(
+                        r_ps[:], w_rot[:, kb, channels], h_sb[:, kb, tokens], start=kb == 0, stop=kb == KB - 1
+                    )
+                t_sb = work.tile([P, PIECE], F32, name="t_sb")
+                nc.scalar.copy(t_sb[:], t_ps[:])
+                r_sb = work.tile([P, PIECE], F32, name="r_sb")
+                nc.scalar.copy(r_sb[:], r_ps[:])
+
+                cos_t = work.tile([P, PIECE], F32, name="cos_t")
+                nc.vector.tensor_tensor(cos_t[:], cos[:].indirect(picked), t_sb[:], MULT)
+                sin_r = work.tile([P, PIECE], F32, name="sin_r")
+                nc.vector.tensor_tensor(sin_r[:], sin[:].indirect(picked), r_sb[:], MULT)
+                turned = work.tile([P, PIECE], F32, name="turned")
+                nc.vector.tensor_tensor(turned[:], cos_t[:], sin_r[:], ADD)
+                nc.sync.dma_start(out[channels, tokens], turned[:])

@@ -5,6 +5,7 @@ H, M, S, N = 256, 256, 2048, 1024
 KB = H // P
 CB = M // P
 PIECE = 512
+PIECES = N // PIECE
 FLOPS = 2 * H * M * N
 
 BF16, F32, U16 = mybir.dt.bfloat16, mybir.dt.float32, mybir.dt.uint16
@@ -15,19 +16,21 @@ def tile_codegenattention_kernel(tc, tab, h, w, offs, out):
     nc = tc.nc
     with (
         tc.tile_pool(name="held", bufs=1) as held,
-        tc.tile_pool(name="work", bufs=2) as work,
+        tc.tile_pool(name="work", bufs=3) as work,
         tc.psum_pool(name="psum", bufs=2) as psum,
     ):
+        h_blocks = h.rearrange("(kb p) j -> p kb j", p=P)
         offsets = held.tile([P, N // 16], U16, name="offsets")
         nc.sync.dma_start(offsets[:], offs)
         w_sb = held.tile([P, KB, M], BF16, name="w_sb")
         nc.sync.dma_start(w_sb[:], w.rearrange("(kb p) c -> p kb c", p=P))
         h_sb = held.tile([P, KB, N], BF16, name="h_sb")
-        nc.sync.dma_start(h_sb[:], h.rearrange("(kb p) j -> p kb j", p=P))
+        nc.sync.dma_start(h_sb[:, :, 0:PIECE], h_blocks[:, :, 0:PIECE])
         cos = held.tile([P, S], F32, name="cos")
-        nc.scalar.dma_start(cos[:], tab[0:P, :])
+        nc.sync.dma_start(cos[:], tab[0:P, :])
+        nc.sync.dma_start(h_sb[:, :, PIECE:N], h_blocks[:, :, PIECE:N])
         sin = held.tile([P, S], F32, name="sin")
-        nc.scalar.dma_start(sin[:], tab[P : 2 * P, :])
+        nc.sync.dma_start(sin[:], tab[P : 2 * P, :])
 
         w_rot = held.tile([P, KB, M], BF16, name="w_rot")
         w_pairs = w_sb[:].rearrange("p kb (i two) -> p kb i two", two=2)
@@ -37,7 +40,7 @@ def tile_codegenattention_kernel(tc, tab, h, w, offs, out):
 
         for cb in range(CB):
             channels = slice(cb * P, (cb + 1) * P)
-            for piece in range(N // PIECE):
+            for piece in range(PIECES):
                 tokens = slice(piece * PIECE, (piece + 1) * PIECE)
                 picked = offsets[:, piece * (PIECE // 16) : (piece + 1) * (PIECE // 16)]
 

@@ -10,14 +10,16 @@ FLOPS = 2 * H * M * N
 
 BF16, F32, U16 = mybir.dt.bfloat16, mybir.dt.float32, mybir.dt.uint16
 MULT, ADD = mybir.AluOpType.mult, mybir.AluOpType.add
+SIN_LAG = 2
+ADD_LAG = 3
 
 
 def tile_codegenattention_kernel(tc, tab, h, w, offs, out):
     nc = tc.nc
     with (
         tc.tile_pool(name="held", bufs=1) as held,
-        tc.tile_pool(name="work", bufs=3) as work,
-        tc.psum_pool(name="psum", bufs=2) as psum,
+        tc.tile_pool(name="work", bufs=ADD_LAG + 1) as work,
+        tc.psum_pool(name="psum", bufs=4) as psum,
     ):
         h_blocks = h.rearrange("(kb p) j -> p kb j", p=P)
         offsets = held.tile([P, N // 16], U16, name="offsets")
@@ -38,31 +40,45 @@ def tile_codegenattention_kernel(tc, tab, h, w, offs, out):
         nc.vector.tensor_scalar_mul(rot_pairs[:, :, :, 0:1], w_pairs[:, :, :, 1:2], -1.0)
         nc.vector.tensor_copy(rot_pairs[:, :, :, 1:2], w_pairs[:, :, :, 0:1])
 
-        for cb in range(CB):
-            channels = slice(cb * P, (cb + 1) * P)
-            for piece in range(PIECES):
-                tokens = slice(piece * PIECE, (piece + 1) * PIECE)
-                picked = offsets[:, piece * (PIECE // 16) : (piece + 1) * (PIECE // 16)]
+        def project(weights, piece, cb, name):
+            product_ps = psum.tile([P, PIECE], F32, name="product_ps")
+            for kb in range(KB):
+                nc.tensor.matmul(
+                    product_ps[:],
+                    weights[:, kb, cb * P : (cb + 1) * P],
+                    h_sb[:, kb, piece * PIECE : (piece + 1) * PIECE],
+                    start=kb == 0,
+                    stop=kb == KB - 1,
+                )
+            product = held.tile([P, PIECE], F32, name=f"{name}{piece}{cb}")
+            nc.scalar.copy(product[:], product_ps[:])
+            return product
 
-                t_ps = psum.tile([P, PIECE], F32, name="t_ps")
-                r_ps = psum.tile([P, PIECE], F32, name="r_ps")
-                for kb in range(KB):
-                    nc.tensor.matmul(
-                        t_ps[:], w_sb[:, kb, channels], h_sb[:, kb, tokens], start=kb == 0, stop=kb == KB - 1
-                    )
-                for kb in range(KB):
-                    nc.tensor.matmul(
-                        r_ps[:], w_rot[:, kb, channels], h_sb[:, kb, tokens], start=kb == 0, stop=kb == KB - 1
-                    )
-                t_sb = work.tile([P, PIECE], F32, name="t_sb")
-                nc.scalar.copy(t_sb[:], t_ps[:])
-                r_sb = work.tile([P, PIECE], F32, name="r_sb")
-                nc.scalar.copy(r_sb[:], r_ps[:])
+        steps = [(piece, cb) for piece in range(PIECES) for cb in range(CB)]
+        t_sb, r_sb = {}, {}
+        for piece in range(PIECES):
+            for cb in range(CB):
+                t_sb[piece, cb] = project(w_sb, piece, cb, "t")
+            for cb in range(CB):
+                r_sb[piece, cb] = project(w_rot, piece, cb, "r")
 
-                cos_t = work.tile([P, PIECE], F32, name="cos_t")
-                nc.vector.tensor_tensor(cos_t[:], cos[:].indirect(picked), t_sb[:], MULT)
-                sin_r = work.tile([P, PIECE], F32, name="sin_r")
-                nc.vector.tensor_tensor(sin_r[:], sin[:].indirect(picked), r_sb[:], MULT)
+        def picked(piece):
+            return offsets[:, piece * (PIECE // 16) : (piece + 1) * (PIECE // 16)]
+
+        cos_t, sin_r = {}, {}
+        for i in range(len(steps) + ADD_LAG):
+            if SIN_LAG <= i < len(steps) + SIN_LAG:
+                piece, cb = steps[i - SIN_LAG]
+                sin_r[piece, cb] = work.tile([P, PIECE], F32, name="sin_r")
+                nc.vector.tensor_tensor(sin_r[piece, cb][:], sin[:].indirect(picked(piece)), r_sb[piece, cb][:], MULT)
+            if i < len(steps):
+                piece, cb = steps[i]
+                cos_t[piece, cb] = work.tile([P, PIECE], F32, name="cos_t")
+                nc.vector.tensor_tensor(cos_t[piece, cb][:], cos[:].indirect(picked(piece)), t_sb[piece, cb][:], MULT)
+            if i >= ADD_LAG:
+                piece, cb = steps[i - ADD_LAG]
                 turned = work.tile([P, PIECE], F32, name="turned")
-                nc.vector.tensor_tensor(turned[:], cos_t[:], sin_r[:], ADD)
-                nc.sync.dma_start(out[channels, tokens], turned[:])
+                nc.vector.tensor_tensor(turned[:], cos_t[piece, cb][:], sin_r[piece, cb][:], ADD)
+                nc.sync.dma_start(
+                    out[cb * P : (cb + 1) * P, piece * PIECE : (piece + 1) * PIECE], turned[:]
+                )

@@ -1,4 +1,5 @@
 import concourse.mybir as mybir
+from concourse.masks import make_identity
 
 P = 128
 H, M, S, N = 256, 256, 2048, 1024
@@ -10,8 +11,8 @@ FLOPS = 2 * H * M * N
 
 BF16, F32, U16 = mybir.dt.bfloat16, mybir.dt.float32, mybir.dt.uint16
 MULT, ADD = mybir.AluOpType.mult, mybir.AluOpType.add
-SIN_LAG = 2
-ADD_LAG = 3
+SIN_LAG = 3
+ADD_LAG = 4
 
 
 def tile_codegenattention_kernel(tc, tab, h, w, offs, out):
@@ -20,6 +21,7 @@ def tile_codegenattention_kernel(tc, tab, h, w, offs, out):
         tc.tile_pool(name="held", bufs=1) as held,
         tc.tile_pool(name="work", bufs=ADD_LAG + 1) as work,
         tc.psum_pool(name="psum", bufs=4) as psum,
+        tc.psum_pool(name="psum_sums", bufs=2) as psum_sums,
     ):
         h_blocks = h.rearrange("(kb p) j -> p kb j", p=P)
         offsets = held.tile([P, N // 16], U16, name="offsets")
@@ -39,6 +41,9 @@ def tile_codegenattention_kernel(tc, tab, h, w, offs, out):
         rot_pairs = w_rot[:].rearrange("p kb (i two) -> p kb i two", two=2)
         nc.vector.tensor_scalar_mul(rot_pairs[:, :, :, 0:1], w_pairs[:, :, :, 1:2], -1.0)
         nc.vector.tensor_copy(rot_pairs[:, :, :, 1:2], w_pairs[:, :, :, 0:1])
+
+        identity = held.tile([P, P], F32, name="identity")
+        make_identity(nc, identity[:])
 
         def project(weights, piece, cb, name):
             product_ps = psum.tile([P, PIECE], F32, name="product_ps")
@@ -78,7 +83,13 @@ def tile_codegenattention_kernel(tc, tab, h, w, offs, out):
             if i >= ADD_LAG:
                 piece, cb = steps[i - ADD_LAG]
                 turned = work.tile([P, PIECE], F32, name="turned")
-                nc.vector.tensor_tensor(turned[:], cos_t[piece, cb][:], sin_r[piece, cb][:], ADD)
+                if piece == 0:
+                    sum_ps = psum_sums.tile([P, PIECE], F32, name="sum_ps")
+                    nc.tensor.matmul(sum_ps[:], identity[:], cos_t[piece, cb][:], start=True, stop=False)
+                    nc.tensor.matmul(sum_ps[:], identity[:], sin_r[piece, cb][:], start=False, stop=True)
+                    nc.scalar.copy(turned[:], sum_ps[:])
+                else:
+                    nc.vector.tensor_tensor(turned[:], cos_t[piece, cb][:], sin_r[piece, cb][:], ADD)
                 nc.sync.dma_start(
                     out[cb * P : (cb + 1) * P, piece * PIECE : (piece + 1) * PIECE], turned[:]
                 )

@@ -11,30 +11,29 @@ FLOPS = 2 * H * M * N
 
 BF16, F32, U16 = mybir.dt.bfloat16, mybir.dt.float32, mybir.dt.uint16
 MULT, ADD = mybir.AluOpType.mult, mybir.AluOpType.add
-SIN_LAG = 3
-ADD_LAG = 4
 
 
 def tile_codegenattention_kernel(tc, tab, h, w, offs, out):
     nc = tc.nc
     with (
         tc.tile_pool(name="held", bufs=1) as held,
-        tc.tile_pool(name="work", bufs=ADD_LAG + 1) as work,
+        tc.tile_pool(name="work", bufs=4) as work,
         tc.psum_pool(name="psum", bufs=4) as psum,
-        tc.psum_pool(name="psum_sums", bufs=2) as psum_sums,
+        tc.psum_pool(name="psum_sums", bufs=1) as psum_sums,
     ):
-        h_blocks = h.rearrange("(kb p) j -> p kb j", p=P)
         offsets = held.tile([P, N // 16], U16, name="offsets")
         nc.sync.dma_start(offsets[:], offs)
         w_sb = held.tile([P, KB, M], BF16, name="w_sb")
         nc.sync.dma_start(w_sb[:], w.rearrange("(kb p) c -> p kb c", p=P))
         h_sb = held.tile([P, KB, N], BF16, name="h_sb")
-        nc.sync.dma_start(h_sb[:, :, 0:PIECE], h_blocks[:, :, 0:PIECE])
+        nc.sync.dma_start(h_sb[:], h.rearrange("(kb p) j -> p kb j", p=P))
         cos = held.tile([P, S], F32, name="cos")
         nc.sync.dma_start(cos[:], tab[0:P, :])
-        nc.sync.dma_start(h_sb[:, :, PIECE:N], h_blocks[:, :, PIECE:N])
         sin = held.tile([P, S], F32, name="sin")
         nc.sync.dma_start(sin[:], tab[P : 2 * P, :])
+
+        identity = held.tile([P, P], F32, name="identity")
+        make_identity(nc, identity[:])
 
         w_rot = held.tile([P, KB, M], BF16, name="w_rot")
         w_pairs = w_sb[:].rearrange("p kb (i two) -> p kb i two", two=2)
@@ -42,10 +41,7 @@ def tile_codegenattention_kernel(tc, tab, h, w, offs, out):
         nc.vector.tensor_scalar_mul(rot_pairs[:, :, :, 0:1], w_pairs[:, :, :, 1:2], -1.0)
         nc.vector.tensor_copy(rot_pairs[:, :, :, 1:2], w_pairs[:, :, :, 0:1])
 
-        identity = held.tile([P, P], F32, name="identity")
-        make_identity(nc, identity[:])
-
-        def project(weights, piece, cb, name):
+        def project(weights, cb, piece, name):
             product_ps = psum.tile([P, PIECE], F32, name="product_ps")
             for kb in range(KB):
                 nc.tensor.matmul(
@@ -59,37 +55,35 @@ def tile_codegenattention_kernel(tc, tab, h, w, offs, out):
             nc.scalar.copy(product[:], product_ps[:])
             return product
 
+        def look_up_times(table, picked, other, name):
+            product = held.tile([P, PIECE], F32, name=name)
+            nc.vector.tensor_tensor(product[:], table[:].indirect(picked), other[:], MULT)
+            return product
+
         steps = [(piece, cb) for piece in range(PIECES) for cb in range(CB)]
-        t_sb, r_sb = {}, {}
-        for piece in range(PIECES):
-            for cb in range(CB):
-                t_sb[piece, cb] = project(w_sb, piece, cb, "t")
-            for cb in range(CB):
-                r_sb[piece, cb] = project(w_rot, piece, cb, "r")
+        picked = [offsets[:, piece * (PIECE // 16) : (piece + 1) * (PIECE // 16)] for piece in range(PIECES)]
 
-        def picked(piece):
-            return offsets[:, piece * (PIECE // 16) : (piece + 1) * (PIECE // 16)]
+        t_sb = [project(w_sb, cb, piece, "t") for piece, cb in steps]
+        r_sb = [project(w_rot, cb, piece, "r") for piece, cb in steps]
 
-        cos_t, sin_r = {}, {}
-        for i in range(len(steps) + ADD_LAG):
-            if SIN_LAG <= i < len(steps) + SIN_LAG:
-                piece, cb = steps[i - SIN_LAG]
-                sin_r[piece, cb] = work.tile([P, PIECE], F32, name="sin_r")
-                nc.vector.tensor_tensor(sin_r[piece, cb][:], sin[:].indirect(picked(piece)), r_sb[piece, cb][:], MULT)
-            if i < len(steps):
-                piece, cb = steps[i]
-                cos_t[piece, cb] = work.tile([P, PIECE], F32, name="cos_t")
-                nc.vector.tensor_tensor(cos_t[piece, cb][:], cos[:].indirect(picked(piece)), t_sb[piece, cb][:], MULT)
-            if i >= ADD_LAG:
-                piece, cb = steps[i - ADD_LAG]
-                turned = work.tile([P, PIECE], F32, name="turned")
-                if piece == 0:
-                    sum_ps = psum_sums.tile([P, PIECE], F32, name="sum_ps")
-                    nc.tensor.matmul(sum_ps[:], identity[:], cos_t[piece, cb][:], start=True, stop=False)
-                    nc.tensor.matmul(sum_ps[:], identity[:], sin_r[piece, cb][:], start=False, stop=True)
-                    nc.scalar.copy(turned[:], sum_ps[:])
-                else:
-                    nc.vector.tensor_tensor(turned[:], cos_t[piece, cb][:], sin_r[piece, cb][:], ADD)
-                nc.sync.dma_start(
-                    out[cb * P : (cb + 1) * P, piece * PIECE : (piece + 1) * PIECE], turned[:]
-                )
+        cos_t = [look_up_times(cos, picked[piece], t_sb[i], f"cos_t{i}") for i, (piece, cb) in enumerate(steps)]
+        sin_r = [look_up_times(sin, picked[piece], r_sb[i], f"sin_r{i}") for i, (piece, cb) in enumerate(steps)]
+
+        def store(i, turned):
+            piece, cb = steps[i]
+            nc.sync.dma_start(out[cb * P : (cb + 1) * P, piece * PIECE : (piece + 1) * PIECE], turned[:])
+
+        on_tensor = range(CB)
+        sum_ps = [psum_sums.tile([P, PIECE], F32, name=f"sum_ps{i}") for i in on_tensor]
+        for i in on_tensor:
+            nc.tensor.matmul(sum_ps[i][:], identity[:], cos_t[i][:], start=True, stop=False)
+        for i in on_tensor:
+            nc.tensor.matmul(sum_ps[i][:], identity[:], sin_r[i][:], start=False, stop=True)
+            turned = work.tile([P, PIECE], F32, name="turned")
+            nc.scalar.copy(turned[:], sum_ps[i][:])
+            store(i, turned)
+
+        for i in range(CB, len(steps)):
+            turned = work.tile([P, PIECE], F32, name="turned")
+            nc.vector.tensor_tensor(turned[:], cos_t[i][:], sin_r[i][:], ADD)
+            store(i, turned)

@@ -25,10 +25,12 @@ def tile_codegenattention_kernel(tc, tab, h, w, offs, out):
         nc.sync.dma_start(offsets[:], offs)
         w_sb = held.tile([P, KB, M], BF16, name="w_sb")
         nc.sync.dma_start(w_sb[:], w.rearrange("(kb p) c -> p kb c", p=P))
+        h_blocks = h.rearrange("(kb p) j -> p kb j", p=P)
         h_sb = held.tile([P, KB, N], BF16, name="h_sb")
-        nc.sync.dma_start(h_sb[:], h.rearrange("(kb p) j -> p kb j", p=P))
+        nc.sync.dma_start(h_sb[:, :, 0:PIECE], h_blocks[:, :, 0:PIECE])
         cos = held.tile([P, S], F32, name="cos")
         nc.sync.dma_start(cos[:], tab[0:P, :])
+        nc.sync.dma_start(h_sb[:, :, PIECE:N], h_blocks[:, :, PIECE:N])
         sin = held.tile([P, S], F32, name="sin")
         nc.sync.dma_start(sin[:], tab[P : 2 * P, :])
 

@@ -17,7 +17,6 @@ def tile_codegenattention_kernel(tc, tab, h, w, offs, out):
     nc = tc.nc
     with (
         tc.tile_pool(name="held", bufs=1) as held,
-        tc.tile_pool(name="work", bufs=4) as work,
         tc.psum_pool(name="psum", bufs=4) as psum,
         tc.psum_pool(name="psum_sums", bufs=1) as psum_sums,
     ):
@@ -71,9 +70,10 @@ def tile_codegenattention_kernel(tc, tab, h, w, offs, out):
         cos_t = [look_up_times(cos, picked[piece], t_sb[i], f"cos_t{i}") for i, (piece, cb) in enumerate(steps)]
         sin_r = [look_up_times(sin, picked[piece], r_sb[i], f"sin_r{i}") for i, (piece, cb) in enumerate(steps)]
 
-        def store(i, turned):
+        def store(queue, i, turned, first=0, width=PIECE):
             piece, cb = steps[i]
-            nc.sync.dma_start(out[cb * P : (cb + 1) * P, piece * PIECE : (piece + 1) * PIECE], turned[:])
+            columns = slice(piece * PIECE + first, piece * PIECE + first + width)
+            queue.dma_start(out[cb * P : (cb + 1) * P, columns], turned[:])
 
         on_tensor = range(CB)
         sum_ps = [psum_sums.tile([P, PIECE], F32, name=f"sum_ps{i}") for i in on_tensor]
@@ -81,11 +81,15 @@ def tile_codegenattention_kernel(tc, tab, h, w, offs, out):
             nc.tensor.matmul(sum_ps[i][:], identity[:], cos_t[i][:], start=True, stop=False)
         for i in on_tensor:
             nc.tensor.matmul(sum_ps[i][:], identity[:], sin_r[i][:], start=False, stop=True)
-            turned = work.tile([P, PIECE], F32, name="turned")
+            turned = held.tile([P, PIECE], F32, name=f"turned{i}")
             nc.scalar.copy(turned[:], sum_ps[i][:])
-            store(i, turned)
+            store(nc.scalar, i, turned)
 
         for i in range(CB, len(steps)):
-            turned = work.tile([P, PIECE], F32, name="turned")
-            nc.vector.tensor_tensor(turned[:], cos_t[i][:], sin_r[i][:], ADD)
-            store(i, turned)
+            width = PIECE if i < len(steps) - 1 else PIECE // 4
+            for first in range(0, PIECE, width):
+                turned = held.tile([P, width], F32, name=f"turned{i}_{first}")
+                nc.vector.tensor_tensor(
+                    turned[:], cos_t[i][:, first : first + width], sin_r[i][:, first : first + width], ADD
+                )
+                store(nc.sync, i, turned, first, width)

@@ -7,6 +7,7 @@ KB = H // P
 CB = M // P
 PIECE = 512
 PIECES = N // PIECE
+HALF = PIECE // 2
 FLOPS = 2 * H * M * N
 
 BF16, F32, U16 = mybir.dt.bfloat16, mybir.dt.float32, mybir.dt.uint16
@@ -17,6 +18,7 @@ def tile_codegenattention_kernel(tc, tab, h, w, offs, out):
     nc = tc.nc
     with (
         tc.tile_pool(name="held", bufs=1) as held,
+        tc.tile_pool(name="sums", bufs=6) as sums,
         tc.psum_pool(name="psum", bufs=4) as psum,
         tc.psum_pool(name="psum_sums", bufs=1) as psum_sums,
     ):
@@ -42,7 +44,10 @@ def tile_codegenattention_kernel(tc, tab, h, w, offs, out):
         nc.vector.tensor_scalar_mul(rot_pairs[:, :, :, 0:1], w_pairs[:, :, :, 1:2], -1.0)
         nc.vector.tensor_copy(rot_pairs[:, :, :, 1:2], w_pairs[:, :, :, 0:1])
 
-        def project(weights, cb, piece, name):
+        steps = [(piece, cb) for piece in range(PIECES) for cb in range(CB)]
+
+        def project(weights, i, name):
+            piece, cb = steps[i]
             product_ps = psum.tile([P, PIECE], F32, name="product_ps")
             for kb in range(KB):
                 nc.tensor.matmul(
@@ -52,44 +57,45 @@ def tile_codegenattention_kernel(tc, tab, h, w, offs, out):
                     start=kb == 0,
                     stop=kb == KB - 1,
                 )
-            product = held.tile([P, PIECE], F32, name=f"{name}{piece}{cb}")
+            product = held.tile([P, PIECE], F32, name=f"{name}{i}")
             nc.scalar.copy(product[:], product_ps[:])
             return product
 
-        def look_up_times(table, picked, other, name):
-            product = held.tile([P, PIECE], F32, name=name)
-            nc.vector.tensor_tensor(product[:], table[:].indirect(picked), other[:], MULT)
-            return product
+        def look_up_times(table, i, first, width, other, product):
+            token = steps[i][0] * PIECE + first
+            picked = offsets[:, token // 16 : (token + width) // 16]
+            columns = slice(first, first + width)
+            nc.vector.tensor_tensor(product[:, columns], table[:].indirect(picked), other[:, columns], MULT)
 
-        steps = [(piece, cb) for piece in range(PIECES) for cb in range(CB)]
-        picked = [offsets[:, piece * (PIECE // 16) : (piece + 1) * (PIECE // 16)] for piece in range(PIECES)]
-
-        t_sb = [project(w_sb, cb, piece, "t") for piece, cb in steps]
-        r_sb = [project(w_rot, cb, piece, "r") for piece, cb in steps]
-
-        cos_t = [look_up_times(cos, picked[piece], t_sb[i], f"cos_t{i}") for i, (piece, cb) in enumerate(steps)]
-        sin_r = [look_up_times(sin, picked[piece], r_sb[i], f"sin_r{i}") for i, (piece, cb) in enumerate(steps)]
-
-        def store(queue, i, turned, first=0, width=PIECE):
+        def store(queue, i, first, width, turned):
             piece, cb = steps[i]
             columns = slice(piece * PIECE + first, piece * PIECE + first + width)
             queue.dma_start(out[cb * P : (cb + 1) * P, columns], turned[:])
 
-        on_tensor = range(CB)
-        sum_ps = [psum_sums.tile([P, PIECE], F32, name=f"sum_ps{i}") for i in on_tensor]
-        for i in on_tensor:
-            nc.tensor.matmul(sum_ps[i][:], identity[:], cos_t[i][:], start=True, stop=False)
-        for i in on_tensor:
-            nc.tensor.matmul(sum_ps[i][:], identity[:], sin_r[i][:], start=False, stop=True)
-            turned = held.tile([P, PIECE], F32, name=f"turned{i}")
-            nc.scalar.copy(turned[:], sum_ps[i][:])
-            store(nc.scalar, i, turned)
+        on_tensor = [(i, first, HALF) for i in range(CB) for first in (0, HALF)]
+        on_vector = [(i, 0, PIECE) for i in range(CB, len(steps))]
 
-        for i in range(CB, len(steps)):
-            width = PIECE if i < len(steps) - 1 else PIECE // 4
-            for first in range(0, PIECE, width):
-                turned = held.tile([P, width], F32, name=f"turned{i}_{first}")
-                nc.vector.tensor_tensor(
-                    turned[:], cos_t[i][:, first : first + width], sin_r[i][:, first : first + width], ADD
-                )
-                store(nc.sync, i, turned, first, width)
+        t_sb = [project(w_sb, i, "t") for i in range(len(steps))]
+        r_sb = [project(w_rot, i, "r") for i in range(len(steps))]
+
+        cos_t = [held.tile([P, PIECE], F32, name=f"cos_t{i}") for i in range(len(steps))]
+        sin_r = [held.tile([P, PIECE], F32, name=f"sin_r{i}") for i in range(len(steps))]
+        for i in range(len(steps)):
+            look_up_times(cos, i, 0, PIECE, t_sb[i], cos_t[i])
+        for i, first, width in on_tensor + on_vector:
+            look_up_times(sin, i, first, width, r_sb[i], sin_r[i])
+
+        sum_ps = [psum_sums.tile([P, width], F32, name=f"sum_ps{i}_{first}") for i, first, width in on_tensor]
+        for (i, first, width), total in zip(on_tensor, sum_ps):
+            nc.tensor.matmul(total[:], identity[:], cos_t[i][:, first : first + width], start=True, stop=False)
+        for (i, first, width), total in zip(on_tensor, sum_ps):
+            nc.tensor.matmul(total[:], identity[:], sin_r[i][:, first : first + width], start=False, stop=True)
+            turned = sums.tile([P, width], F32, name="turned")
+            nc.scalar.copy(turned[:], total[:])
+            store(nc.sync, i, first, width, turned)
+
+        for i, first, width in on_vector:
+            turned = sums.tile([P, width], F32, name="turned")
+            columns = slice(first, first + width)
+            nc.vector.tensor_tensor(turned[:], cos_t[i][:, columns], sin_r[i][:, columns], ADD)
+            store(nc.sync, i, first, width, turned)

@@ -18,8 +18,8 @@ def tile_codegenattention_kernel(tc, tab, h, w, offs, out):
     nc = tc.nc
     with (
         tc.tile_pool(name="held", bufs=1) as held,
-        tc.tile_pool(name="sums", bufs=6) as sums,
-        tc.psum_pool(name="psum", bufs=4) as psum,
+        tc.tile_pool(name="sums", bufs=7) as sums,
+        tc.psum_pool(name="psum", bufs=3) as psum,
         tc.psum_pool(name="psum_sums", bufs=1) as psum_sums,
     ):
         offsets = held.tile([P, N // 16], U16, name="offsets")
@@ -72,8 +72,8 @@ def tile_codegenattention_kernel(tc, tab, h, w, offs, out):
             columns = slice(piece * PIECE + first, piece * PIECE + first + width)
             queue.dma_start(out[cb * P : (cb + 1) * P, columns], turned[:])
 
-        on_tensor = [(i, first, HALF) for i in range(CB) for first in (0, HALF)]
-        on_vector = [(i, 0, PIECE) for i in range(CB, len(steps))]
+        on_tensor = [(i, first, HALF) for i in range(CB) for first in (0, HALF)] + [(CB, 0, HALF)]
+        on_vector = [(CB, HALF, HALF), (CB + 1, 0, PIECE)]
 
         t_sb = [project(w_sb, i, "t") for i in range(len(steps))]
         r_sb = [project(w_rot, i, "r") for i in range(len(steps))]

@@ -12,15 +12,15 @@ FLOPS = 2 * H * M * N
 
 BF16, F32, U16 = mybir.dt.bfloat16, mybir.dt.float32, mybir.dt.uint16
 MULT, ADD = mybir.AluOpType.mult, mybir.AluOpType.add
+IDENTITY = mybir.ActivationFunctionType.Identity
 
 
 def tile_codegenattention_kernel(tc, tab, h, w, offs, out):
     nc = tc.nc
     with (
         tc.tile_pool(name="held", bufs=1) as held,
-        tc.tile_pool(name="sums", bufs=7) as sums,
-        tc.psum_pool(name="psum", bufs=3) as psum,
-        tc.psum_pool(name="psum_sums", bufs=1) as psum_sums,
+        tc.tile_pool(name="turned", bufs=6) as sums,
+        tc.psum_pool(name="psum", bufs=8) as psum,
     ):
         offsets = held.tile([P, N // 16], U16, name="offsets")
         nc.sync.dma_start(offsets[:], offs)
@@ -33,33 +33,43 @@ def tile_codegenattention_kernel(tc, tab, h, w, offs, out):
         nc.sync.dma_start(cos[:], tab[0:P, :])
         nc.sync.dma_start(h_sb[:, :, PIECE:N], h_blocks[:, :, PIECE:N])
         sin = held.tile([P, S], F32, name="sin")
-        nc.sync.dma_start(sin[:], tab[P : 2 * P, :])
+        nc.sync.dma_start(sin[1:P:2, :], tab[P : 2 * P : 2, :])
+        nc.sync.dma_start(sin[0:P:2, :], tab[P + 1 : 2 * P : 2, :])
 
-        identity = held.tile([P, P], F32, name="identity")
-        make_identity(nc, identity[:])
+        home = held.tile([P, P], F32, name="home")
+        make_identity(nc, home[:])
+        swap = held.tile([P, P], F32, name="swap")
+        home_pairs = home[:].rearrange("p (i two) -> p i two", two=2)
+        swap_pairs = swap[:].rearrange("p (i two) -> p i two", two=2)
+        nc.gpsimd.tensor_copy(swap_pairs[:, :, 0:1], home_pairs[:, :, 1:2])
+        nc.gpsimd.tensor_copy(swap_pairs[:, :, 1:2], home_pairs[:, :, 0:1])
 
-        w_rot = held.tile([P, KB, M], BF16, name="w_rot")
-        w_pairs = w_sb[:].rearrange("p kb (i two) -> p kb i two", two=2)
-        rot_pairs = w_rot[:].rearrange("p kb (i two) -> p kb i two", two=2)
-        nc.vector.tensor_scalar_mul(rot_pairs[:, :, :, 0:1], w_pairs[:, :, :, 1:2], -1.0)
-        nc.vector.tensor_copy(rot_pairs[:, :, :, 1:2], w_pairs[:, :, :, 0:1])
+        width = P // 4
+        folded = held.tile([P, width], F32, name="folded")
+        nc.gpsimd.tensor_tensor(folded[:], home[:, 0 : P // 2 : 2], home[:, P // 2 : P : 2], ADD)
+        while width > 1:
+            width //= 2
+            nc.gpsimd.tensor_tensor(folded[:, 0:width], folded[:, 0:width], folded[:, width : 2 * width], ADD)
+        sign = held.tile([P, 1], F32, name="sign")
+        nc.gpsimd.tensor_scalar(sign[:], folded[:, 0:1], 2.0, -1.0, MULT, ADD)
 
         steps = [(piece, cb) for piece in range(PIECES) for cb in range(CB)]
 
-        def project(weights, i, name):
-            piece, cb = steps[i]
-            product_ps = psum.tile([P, PIECE], F32, name="product_ps")
+        t_sb, r_sb = [], []
+        for i, (piece, cb) in enumerate(steps):
+            t_ps = psum.tile([P, PIECE], F32, name="t_ps", tag="bank")
             for kb in range(KB):
                 nc.tensor.matmul(
-                    product_ps[:],
-                    weights[:, kb, cb * P : (cb + 1) * P],
+                    t_ps[:],
+                    w_sb[:, kb, cb * P : (cb + 1) * P],
                     h_sb[:, kb, piece * PIECE : (piece + 1) * PIECE],
                     start=kb == 0,
                     stop=kb == KB - 1,
                 )
-            product = held.tile([P, PIECE], F32, name=f"{name}{i}")
-            nc.scalar.copy(product[:], product_ps[:])
-            return product
+            t_sb.append(held.tile([P, PIECE], F32, name=f"t{i}"))
+            nc.scalar.copy(t_sb[i][:], t_ps[:])
+            r_sb.append(held.tile([P, PIECE], F32, name=f"r{i}"))
+            nc.scalar.activation(r_sb[i][:], t_ps[:], IDENTITY, scale=sign[:])
 
         def look_up_times(table, i, first, width, other, product):
             token = steps[i][0] * PIECE + first
@@ -67,35 +77,35 @@ def tile_codegenattention_kernel(tc, tab, h, w, offs, out):
             columns = slice(first, first + width)
             nc.vector.tensor_tensor(product[:, columns], table[:].indirect(picked), other[:, columns], MULT)
 
-        def store(queue, i, first, width, turned):
-            piece, cb = steps[i]
-            columns = slice(piece * PIECE + first, piece * PIECE + first + width)
-            queue.dma_start(out[cb * P : (cb + 1) * P, columns], turned[:])
-
-        on_tensor = [(i, first, HALF) for i in range(CB) for first in (0, HALF)] + [(CB, 0, HALF)]
-        on_vector = [(CB, HALF, HALF), (CB + 1, 0, PIECE)]
-
-        t_sb = [project(w_sb, i, "t") for i in range(len(steps))]
-        r_sb = [project(w_rot, i, "r") for i in range(len(steps))]
-
         cos_t = [held.tile([P, PIECE], F32, name=f"cos_t{i}") for i in range(len(steps))]
         sin_r = [held.tile([P, PIECE], F32, name=f"sin_r{i}") for i in range(len(steps))]
-        for i in range(len(steps)):
+        last = len(steps) - 1
+        for i in range(last):
             look_up_times(cos, i, 0, PIECE, t_sb[i], cos_t[i])
-        for i, first, width in on_tensor + on_vector:
-            look_up_times(sin, i, first, width, r_sb[i], sin_r[i])
+        for i in range(last):
+            look_up_times(sin, i, 0, PIECE, r_sb[i], sin_r[i])
+        look_up_times(cos, last, 0, PIECE, t_sb[last], cos_t[last])
+        for first in (0, HALF):
+            look_up_times(sin, last, first, HALF, r_sb[last], sin_r[last])
 
-        sum_ps = [psum_sums.tile([P, width], F32, name=f"sum_ps{i}_{first}") for i, first, width in on_tensor]
-        for (i, first, width), total in zip(on_tensor, sum_ps):
-            nc.tensor.matmul(total[:], identity[:], cos_t[i][:, first : first + width], start=True, stop=False)
-        for (i, first, width), total in zip(on_tensor, sum_ps):
-            nc.tensor.matmul(total[:], identity[:], sin_r[i][:, first : first + width], start=False, stop=True)
-            turned = sums.tile([P, width], F32, name="turned")
+        for i, first in [(i, first) for i in range(last) for first in (0, HALF)]:
+            columns = slice(first, first + HALF)
+            total = psum.tile([P, HALF], F32, name="total", tag="bank")
+            nc.tensor.matmul(total[:], home[:], cos_t[i][:, columns], start=True, stop=False)
+            nc.tensor.matmul(total[:], swap[:], sin_r[i][:, columns], start=False, stop=True)
+            turned = sums.tile([P, HALF], F32, name="turned")
             nc.scalar.copy(turned[:], total[:])
-            store(nc.sync, i, first, width, turned)
+            piece, cb = steps[i]
+            token = piece * PIECE + first
+            nc.sync.dma_start(out[cb * P : (cb + 1) * P, token : token + HALF], turned[:])
 
-        for i, first, width in on_vector:
-            turned = sums.tile([P, width], F32, name="turned")
-            columns = slice(first, first + width)
-            nc.vector.tensor_tensor(turned[:], cos_t[i][:, columns], sin_r[i][:, columns], ADD)
-            store(nc.sync, i, first, width, turned)
+        moved = psum.tile([P, PIECE], F32, name="moved", tag="bank")
+        nc.tensor.matmul(moved[:], swap[:], cos_t[last][:], start=True, stop=True)
+        last_turned = held.tile([P, PIECE], F32, name="last_turned")
+        for first in (0, HALF):
+            columns = slice(first, first + HALF)
+            nc.vector.tensor_tensor(last_turned[:, columns], moved[:, columns], sin_r[last][:, columns], ADD)
+        piece, cb = steps[last]
+        tokens = slice(piece * PIECE, (piece + 1) * PIECE)
+        nc.sync.dma_start(out[cb * P : (cb + 1) * P : 2, tokens], last_turned[1:P:2, :])
+        nc.sync.dma_start(out[cb * P + 1 : (cb + 1) * P : 2, tokens], last_turned[0:P:2, :])

@@ -69,7 +69,7 @@ def tile_codegenattention_kernel(tc, tab, h, w, offs, out):
             t_sb.append(held.tile([P, PIECE], F32, name=f"t{i}"))
             nc.scalar.copy(t_sb[i][:], t_ps[:])
             r_sb.append(held.tile([P, PIECE], F32, name=f"r{i}"))
-            nc.scalar.activation(r_sb[i][:], t_ps[:], IDENTITY, scale=sign[:])
+            nc.scalar.activation(r_sb[i][:], t_sb[i][:], IDENTITY, scale=sign[:])
 
         def look_up_times(table, i, first, width, other, product):
             token = steps[i][0] * PIECE + first
@@ -82,11 +82,12 @@ def tile_codegenattention_kernel(tc, tab, h, w, offs, out):
         last = len(steps) - 1
         for i in range(last):
             look_up_times(cos, i, 0, PIECE, t_sb[i], cos_t[i])
-        for i in range(last):
+        for i in range(last - 1):
             look_up_times(sin, i, 0, PIECE, r_sb[i], sin_r[i])
         look_up_times(cos, last, 0, PIECE, t_sb[last], cos_t[last])
-        for first in (0, HALF):
-            look_up_times(sin, last, first, HALF, r_sb[last], sin_r[last])
+        for i in (last - 1, last):
+            for first in (0, HALF):
+                look_up_times(sin, i, first, HALF, r_sb[i], sin_r[i])
 
         for i, first in [(i, first) for i in range(last) for first in (0, HALF)]:
             columns = slice(first, first + HALF)

@@ -19,7 +19,7 @@ def tile_codegenattention_kernel(tc, tab, h, w, offs, out):
     nc = tc.nc
     with (
         tc.tile_pool(name="held", bufs=1) as held,
-        tc.tile_pool(name="turned", bufs=6) as sums,
+        tc.tile_pool(name="sums", bufs=4) as sums,
         tc.psum_pool(name="psum", bufs=8) as psum,
     ):
         offsets = held.tile([P, N // 16], U16, name="offsets")
@@ -89,24 +89,36 @@ def tile_codegenattention_kernel(tc, tab, h, w, offs, out):
             for first in (0, HALF):
                 look_up_times(sin, i, first, HALF, r_sb[i], sin_r[i])
 
-        for i, first in [(i, first) for i in range(last) for first in (0, HALF)]:
-            columns = slice(first, first + HALF)
-            total = psum.tile([P, HALF], F32, name="total", tag="bank")
-            nc.tensor.matmul(total[:], home[:], cos_t[i][:, columns], start=True, stop=False)
-            nc.tensor.matmul(total[:], swap[:], sin_r[i][:, columns], start=False, stop=True)
-            turned = sums.tile([P, HALF], F32, name="turned")
-            nc.scalar.copy(turned[:], total[:])
-            piece, cb = steps[i]
-            token = piece * PIECE + first
-            nc.sync.dma_start(out[cb * P : (cb + 1) * P, token : token + HALF], turned[:])
+        totals = {}
+        for i in range(last):
+            for first in (0, HALF):
+                total = psum.tile([P, HALF], F32, name="total", tag="bank")
+                nc.tensor.matmul(total[:], home[:], cos_t[i][:, first : first + HALF], start=True, stop=False)
+                totals[i, first] = total
 
         moved = psum.tile([P, PIECE], F32, name="moved", tag="bank")
         nc.tensor.matmul(moved[:], swap[:], cos_t[last][:], start=True, stop=True)
-        last_turned = held.tile([P, PIECE], F32, name="last_turned")
+
+        def close_sum(i, first, turned):
+            total = totals[i, first]
+            nc.tensor.matmul(total[:], swap[:], sin_r[i][:, first : first + HALF], start=False, stop=True)
+            nc.scalar.copy(turned, total[:])
+
+        for i, (piece, cb) in enumerate(steps[: last - 1]):
+            turned = sums.tile([P, PIECE], F32, name="turned")
+            for first in (0, HALF):
+                close_sum(i, first, turned[:, first : first + HALF])
+            nc.sync.dma_start(out[cb * P : (cb + 1) * P, piece * PIECE : (piece + 1) * PIECE], turned[:])
+
+        piece = steps[last][0]
         for first in (0, HALF):
+            tokens = slice(piece * PIECE + first, piece * PIECE + first + HALF)
+            turned_half = sums.tile([P, HALF], F32, name="turned_half")
+            close_sum(last - 1, first, turned_half[:])
+            nc.sync.dma_start(out[0:P, tokens], turned_half[:])
+
             columns = slice(first, first + HALF)
-            nc.vector.tensor_tensor(last_turned[:, columns], moved[:, columns], sin_r[last][:, columns], ADD)
-        piece, cb = steps[last]
-        tokens = slice(piece * PIECE, (piece + 1) * PIECE)
-        nc.sync.dma_start(out[cb * P : (cb + 1) * P : 2, tokens], last_turned[1:P:2, :])
-        nc.sync.dma_start(out[cb * P + 1 : (cb + 1) * P : 2, tokens], last_turned[0:P:2, :])
+            turned_half = sums.tile([P, HALF], F32, name="turned_half")
+            nc.vector.tensor_tensor(turned_half[:], moved[:, columns], sin_r[last][:, columns], ADD)
+            nc.sync.dma_start(out[P : 2 * P : 2, tokens], turned_half[1:P:2, :])
+            nc.sync.dma_start(out[P + 1 : 2 * P : 2, tokens], turned_half[0:P:2, :])

@@ -55,8 +55,13 @@ def tile_codegenattention_kernel(tc, tab, h, w, offs, out):
 
         steps = [(piece, cb) for piece in range(PIECES) for cb in range(CB)]
 
-        t_sb, r_sb = [], []
-        for i, (piece, cb) in enumerate(steps):
+        t_sb = [held.tile([P, PIECE], F32, name=f"t{i}") for i in range(len(steps))]
+        r_sb = [held.tile([P, PIECE], F32, name=f"r{i}") for i in range(len(steps))]
+        cos_t = [held.tile([P, PIECE], F32, name=f"cos_t{i}") for i in range(len(steps))]
+        sin_r = [held.tile([P, PIECE], F32, name=f"sin_r{i}") for i in range(len(steps))]
+
+        def project(i):
+            piece, cb = steps[i]
             t_ps = psum.tile([P, PIECE], F32, name="t_ps", tag="bank")
             for kb in range(KB):
                 nc.tensor.matmul(
@@ -66,9 +71,7 @@ def tile_codegenattention_kernel(tc, tab, h, w, offs, out):
                     start=kb == 0,
                     stop=kb == KB - 1,
                 )
-            t_sb.append(held.tile([P, PIECE], F32, name=f"t{i}"))
             nc.scalar.copy(t_sb[i][:], t_ps[:])
-            r_sb.append(held.tile([P, PIECE], F32, name=f"r{i}"))
             nc.scalar.activation(r_sb[i][:], t_sb[i][:], IDENTITY, scale=sign[:])
 
         def look_up_times(table, i, first, width, other, product):
@@ -77,48 +80,46 @@ def tile_codegenattention_kernel(tc, tab, h, w, offs, out):
             columns = slice(first, first + width)
             nc.vector.tensor_tensor(product[:, columns], table[:].indirect(picked), other[:, columns], MULT)
 
-        cos_t = [held.tile([P, PIECE], F32, name=f"cos_t{i}") for i in range(len(steps))]
-        sin_r = [held.tile([P, PIECE], F32, name=f"sin_r{i}") for i in range(len(steps))]
-        last = len(steps) - 1
-        for i in range(last):
-            look_up_times(cos, i, 0, PIECE, t_sb[i], cos_t[i])
-        for i in range(last - 1):
-            look_up_times(sin, i, 0, PIECE, r_sb[i], sin_r[i])
-        look_up_times(cos, last, 0, PIECE, t_sb[last], cos_t[last])
-        for i in (last - 1, last):
-            for first in (0, HALF):
-                look_up_times(sin, i, first, HALF, r_sb[i], sin_r[i])
-
         totals = {}
-        for i in range(last):
+
+        def open_sums(i):
             for first in (0, HALF):
                 total = psum.tile([P, HALF], F32, name="total", tag="bank")
                 nc.tensor.matmul(total[:], home[:], cos_t[i][:, first : first + HALF], start=True, stop=False)
                 totals[i, first] = total
-
-        moved = psum.tile([P, PIECE], F32, name="moved", tag="bank")
-        nc.tensor.matmul(moved[:], swap[:], cos_t[last][:], start=True, stop=True)
 
         def close_sum(i, first, turned):
             total = totals[i, first]
             nc.tensor.matmul(total[:], swap[:], sin_r[i][:, first : first + HALF], start=False, stop=True)
             nc.scalar.copy(turned, total[:])
 
-        for i, (piece, cb) in enumerate(steps[: last - 1]):
+        last = len(steps) - 1
+        for i in range(last):
+            project(i)
+            look_up_times(cos, i, 0, PIECE, t_sb[i], cos_t[i])
+        for i in range(last - 1):
+            open_sums(i)
+
+        project(last)
+        for i in range(last):
+            look_up_times(sin, i, 0, PIECE, r_sb[i], sin_r[i])
+        open_sums(last - 1)
+        for i, (piece, cb) in enumerate(steps[:last]):
             turned = sums.tile([P, PIECE], F32, name="turned")
             for first in (0, HALF):
                 close_sum(i, first, turned[:, first : first + HALF])
             nc.sync.dma_start(out[cb * P : (cb + 1) * P, piece * PIECE : (piece + 1) * PIECE], turned[:])
 
-        piece = steps[last][0]
+        look_up_times(cos, last, 0, PIECE, t_sb[last], cos_t[last])
         for first in (0, HALF):
-            tokens = slice(piece * PIECE + first, piece * PIECE + first + HALF)
-            turned_half = sums.tile([P, HALF], F32, name="turned_half")
-            close_sum(last - 1, first, turned_half[:])
-            nc.sync.dma_start(out[0:P, tokens], turned_half[:])
-
+            look_up_times(sin, last, first, HALF, r_sb[last], sin_r[last])
+        piece, cb = steps[last]
+        for first in (0, HALF):
             columns = slice(first, first + HALF)
+            moved = psum.tile([P, HALF], F32, name="moved", tag="bank")
+            nc.tensor.matmul(moved[:], swap[:], cos_t[last][:, columns], start=True, stop=True)
             turned_half = sums.tile([P, HALF], F32, name="turned_half")
-            nc.vector.tensor_tensor(turned_half[:], moved[:, columns], sin_r[last][:, columns], ADD)
-            nc.sync.dma_start(out[P : 2 * P : 2, tokens], turned_half[1:P:2, :])
-            nc.sync.dma_start(out[P + 1 : 2 * P : 2, tokens], turned_half[0:P:2, :])
+            nc.vector.tensor_tensor(turned_half[:], moved[:], sin_r[last][:, columns], ADD)
+            tokens = slice(piece * PIECE + first, piece * PIECE + first + HALF)
+            nc.sync.dma_start(out[cb * P : (cb + 1) * P : 2, tokens], turned_half[1:P:2, :])
+            nc.sync.dma_start(out[cb * P + 1 : (cb + 1) * P : 2, tokens], turned_half[0:P:2, :])

@@ -19,7 +19,7 @@ def tile_codegenattention_kernel(tc, tab, h, w, offs, out):
     nc = tc.nc
     with (
         tc.tile_pool(name="held", bufs=1) as held,
-        tc.tile_pool(name="sums", bufs=4) as sums,
+        tc.tile_pool(name="sums", bufs=8) as sums,
         tc.psum_pool(name="psum", bufs=8) as psum,
     ):
         offsets = held.tile([P, N // 16], U16, name="offsets")
@@ -32,9 +32,17 @@ def tile_codegenattention_kernel(tc, tab, h, w, offs, out):
         cos = held.tile([P, S], F32, name="cos")
         nc.sync.dma_start(cos[:], tab[0:P, :])
         nc.sync.dma_start(h_sb[:, :, PIECE:N], h_blocks[:, :, PIECE:N])
+        sin_crossed = held.tile([P, S], F32, name="sin_crossed")
+        nc.sync.dma_start(sin_crossed[1:P:2, :], tab[P : 2 * P : 2, :])
+        nc.sync.dma_start(sin_crossed[0:P:2, :], tab[P + 1 : 2 * P : 2, :])
         sin = held.tile([P, S], F32, name="sin")
-        nc.sync.dma_start(sin[1:P:2, :], tab[P : 2 * P : 2, :])
-        nc.sync.dma_start(sin[0:P:2, :], tab[P + 1 : 2 * P : 2, :])
+        nc.sync.dma_start(sin[:], tab[P : 2 * P, :])
+
+        w_rot = held.tile([P, KB, P], BF16, name="w_rot")
+        w_pairs = w_sb[:, :, M - P : M].rearrange("p kb (i two) -> p kb i two", two=2)
+        rot_pairs = w_rot[:].rearrange("p kb (i two) -> p kb i two", two=2)
+        nc.vector.tensor_scalar_mul(rot_pairs[:, :, :, 0:1], w_pairs[:, :, :, 1:2], -1.0)
+        nc.vector.tensor_copy(rot_pairs[:, :, :, 1:2], w_pairs[:, :, :, 0:1])
 
         home = held.tile([P, P], F32, name="home")
         make_identity(nc, home[:])
@@ -60,19 +68,22 @@ def tile_codegenattention_kernel(tc, tab, h, w, offs, out):
         cos_t = [held.tile([P, PIECE], F32, name=f"cos_t{i}") for i in range(len(steps))]
         sin_r = [held.tile([P, PIECE], F32, name=f"sin_r{i}") for i in range(len(steps))]
 
-        def project(i):
-            piece, cb = steps[i]
-            t_ps = psum.tile([P, PIECE], F32, name="t_ps", tag="bank")
+        def project(weights, i):
+            piece = steps[i][0]
+            product = psum.tile([P, PIECE], F32, name="product", tag="bank")
             for kb in range(KB):
                 nc.tensor.matmul(
-                    t_ps[:],
-                    w_sb[:, kb, cb * P : (cb + 1) * P],
+                    product[:],
+                    weights[:, kb, :],
                     h_sb[:, kb, piece * PIECE : (piece + 1) * PIECE],
                     start=kb == 0,
                     stop=kb == KB - 1,
                 )
-            nc.scalar.copy(t_sb[i][:], t_ps[:])
-            nc.scalar.activation(r_sb[i][:], t_sb[i][:], IDENTITY, scale=sign[:])
+            return product
+
+        def make_t(i):
+            cb = steps[i][1]
+            nc.scalar.copy(t_sb[i][:], project(w_sb[:, :, cb * P : (cb + 1) * P], i)[:])
 
         def look_up_times(table, i, first, width, other, product):
             token = steps[i][0] * PIECE + first
@@ -93,33 +104,35 @@ def tile_codegenattention_kernel(tc, tab, h, w, offs, out):
             nc.tensor.matmul(total[:], swap[:], sin_r[i][:, first : first + HALF], start=False, stop=True)
             nc.scalar.copy(turned, total[:])
 
+        def out_columns(i, first):
+            piece, cb = steps[i]
+            token = piece * PIECE + first
+            return out[cb * P : (cb + 1) * P, token : token + HALF]
+
         last = len(steps) - 1
         for i in range(last):
-            project(i)
+            make_t(i)
+            nc.scalar.activation(r_sb[i][:], t_sb[i][:], IDENTITY, scale=sign[:])
             look_up_times(cos, i, 0, PIECE, t_sb[i], cos_t[i])
+        last_r_ps = project(w_rot[:], last)
         for i in range(last - 1):
             open_sums(i)
 
-        project(last)
+        make_t(last)
+        nc.scalar.copy(r_sb[last][:], last_r_ps[:])
         for i in range(last):
-            look_up_times(sin, i, 0, PIECE, r_sb[i], sin_r[i])
+            look_up_times(sin_crossed, i, 0, PIECE, r_sb[i], sin_r[i])
         open_sums(last - 1)
-        for i, (piece, cb) in enumerate(steps[:last]):
-            turned = sums.tile([P, PIECE], F32, name="turned")
-            for first in (0, HALF):
-                close_sum(i, first, turned[:, first : first + HALF])
-            nc.sync.dma_start(out[cb * P : (cb + 1) * P, piece * PIECE : (piece + 1) * PIECE], turned[:])
+        for i, first in [(i, first) for i in range(last) for first in (0, HALF)]:
+            turned = sums.tile([P, HALF], F32, name="turned")
+            close_sum(i, first, turned[:])
+            nc.sync.dma_start(out_columns(i, first), turned[:])
 
         look_up_times(cos, last, 0, PIECE, t_sb[last], cos_t[last])
         for first in (0, HALF):
             look_up_times(sin, last, first, HALF, r_sb[last], sin_r[last])
-        piece, cb = steps[last]
         for first in (0, HALF):
             columns = slice(first, first + HALF)
-            moved = psum.tile([P, HALF], F32, name="moved", tag="bank")
-            nc.tensor.matmul(moved[:], swap[:], cos_t[last][:, columns], start=True, stop=True)
-            turned_half = sums.tile([P, HALF], F32, name="turned_half")
-            nc.vector.tensor_tensor(turned_half[:], moved[:], sin_r[last][:, columns], ADD)
-            tokens = slice(piece * PIECE + first, piece * PIECE + first + HALF)
-            nc.sync.dma_start(out[cb * P : (cb + 1) * P : 2, tokens], turned_half[1:P:2, :])
-            nc.sync.dma_start(out[cb * P + 1 : (cb + 1) * P : 2, tokens], turned_half[0:P:2, :])
+            turned = sums.tile([P, HALF], F32, name="turned")
+            nc.vector.tensor_tensor(turned[:], cos_t[last][:, columns], sin_r[last][:, columns], ADD)
+            nc.scalar.dma_start(out_columns(last, first), turned[:])

@@ -135,4 +135,4 @@ def tile_codegenattention_kernel(tc, tab, h, w, offs, out):
             columns = slice(first, first + HALF)
             turned = sums.tile([P, HALF], F32, name="turned")
             nc.vector.tensor_tensor(turned[:], cos_t[last][:, columns], sin_r[last][:, columns], ADD)
-            nc.scalar.dma_start(out_columns(last, first), turned[:])
+            nc.sync.dma_start(out_columns(last, first), turned[:])

@@ -25,8 +25,8 @@ def tile_codegenattention_kernel(tc, tab, h, w, offs, out):
         offsets = held.tile([P, N // 16], U16, name="offsets")
         nc.sync.dma_start(offsets[:], offs)
         w_sb = held.tile([P, KB, M], BF16, name="w_sb")
-        nc.sync.dma_start(w_sb[:], w.rearrange("(kb p) c -> p kb c", p=P))
-        h_blocks = h.rearrange("(kb p) j -> p kb j", p=P)
+        nc.sync.dma_start(w_sb[:], w.rearrange("(p kb) c -> p kb c", kb=KB))
+        h_blocks = h.rearrange("(p kb) j -> p kb j", kb=KB)
         h_sb = held.tile([P, KB, N], BF16, name="h_sb")
         nc.sync.dma_start(h_sb[:, :, 0:PIECE], h_blocks[:, :, 0:PIECE])
         cos = held.tile([P, S], F32, name="cos")
@@ -128,11 +128,16 @@ def tile_codegenattention_kernel(tc, tab, h, w, offs, out):
             close_sum(i, first, turned[:])
             nc.sync.dma_start(out_columns(i, first), turned[:])
 
-        look_up_times(cos, last, 0, PIECE, t_sb[last], cos_t[last])
-        for first in (0, HALF):
-            look_up_times(sin, last, first, HALF, r_sb[last], sin_r[last])
-        for first in (0, HALF):
+        look_up_times(cos, last, 0, HALF, t_sb[last], cos_t[last])
+        look_up_times(sin, last, 0, HALF, r_sb[last], sin_r[last])
+        look_up_times(cos, last, HALF, HALF, t_sb[last], cos_t[last])
+
+        def add_on_vector(first):
             columns = slice(first, first + HALF)
             turned = sums.tile([P, HALF], F32, name="turned")
             nc.vector.tensor_tensor(turned[:], cos_t[last][:, columns], sin_r[last][:, columns], ADD)
             nc.sync.dma_start(out_columns(last, first), turned[:])
+
+        add_on_vector(0)
+        look_up_times(sin, last, HALF, HALF, r_sb[last], sin_r[last])
+        add_on_vector(HALF)

import concourse.mybir as mybir
from concourse.masks import make_identity

P = 128
H, M, S, N = 256, 256, 2048, 1024
KB = H // P
CB = M // P
PIECE = 512
PIECES = N // PIECE
HALF = PIECE // 2
FLOPS = 2 * H * M * N

BF16, F32, U16 = mybir.dt.bfloat16, mybir.dt.float32, mybir.dt.uint16
MULT, ADD = mybir.AluOpType.mult, mybir.AluOpType.add
IDENTITY = mybir.ActivationFunctionType.Identity


def tile_codegenattention_kernel(tc, tab, h, w, offs, out):
    nc = tc.nc
    with (
        tc.tile_pool(name="held", bufs=1) as held,
        tc.tile_pool(name="sums", bufs=8) as sums,
        tc.psum_pool(name="psum", bufs=8) as psum,
    ):
        offsets = held.tile([P, N // 16], U16, name="offsets")
        nc.sync.dma_start(offsets[:], offs)
        w_sb = held.tile([P, KB, M], BF16, name="w_sb")
        nc.sync.dma_start(w_sb[:], w.rearrange("(p kb) c -> p kb c", kb=KB))
        h_blocks = h.rearrange("(p kb) j -> p kb j", kb=KB)
        h_sb = held.tile([P, KB, N], BF16, name="h_sb")
        nc.sync.dma_start(h_sb[:, :, 0:PIECE], h_blocks[:, :, 0:PIECE])
        cos = held.tile([P, S], F32, name="cos")
        nc.sync.dma_start(cos[:], tab[0:P, :])
        nc.sync.dma_start(h_sb[:, :, PIECE:N], h_blocks[:, :, PIECE:N])
        sin_crossed = held.tile([P, S], F32, name="sin_crossed")
        nc.sync.dma_start(sin_crossed[1:P:2, :], tab[P : 2 * P : 2, :])
        nc.sync.dma_start(sin_crossed[0:P:2, :], tab[P + 1 : 2 * P : 2, :])
        sin = held.tile([P, S], F32, name="sin")
        nc.sync.dma_start(sin[:], tab[P : 2 * P, :])

        w_rot = held.tile([P, KB, P], BF16, name="w_rot")
        w_pairs = w_sb[:, :, M - P : M].rearrange("p kb (i two) -> p kb i two", two=2)
        rot_pairs = w_rot[:].rearrange("p kb (i two) -> p kb i two", two=2)
        nc.vector.tensor_scalar_mul(rot_pairs[:, :, :, 0:1], w_pairs[:, :, :, 1:2], -1.0)
        nc.vector.tensor_copy(rot_pairs[:, :, :, 1:2], w_pairs[:, :, :, 0:1])

        home = held.tile([P, P], F32, name="home")
        make_identity(nc, home[:])
        swap = held.tile([P, P], F32, name="swap")
        home_pairs = home[:].rearrange("p (i two) -> p i two", two=2)
        swap_pairs = swap[:].rearrange("p (i two) -> p i two", two=2)
        nc.gpsimd.tensor_copy(swap_pairs[:, :, 0:1], home_pairs[:, :, 1:2])
        nc.gpsimd.tensor_copy(swap_pairs[:, :, 1:2], home_pairs[:, :, 0:1])

        width = P // 4
        folded = held.tile([P, width], F32, name="folded")
        nc.gpsimd.tensor_tensor(folded[:], home[:, 0 : P // 2 : 2], home[:, P // 2 : P : 2], ADD)
        while width > 1:
            width //= 2
            nc.gpsimd.tensor_tensor(folded[:, 0:width], folded[:, 0:width], folded[:, width : 2 * width], ADD)
        sign = held.tile([P, 1], F32, name="sign")
        nc.gpsimd.tensor_scalar(sign[:], folded[:, 0:1], 2.0, -1.0, MULT, ADD)

        steps = [(piece, cb) for piece in range(PIECES) for cb in range(CB)]

        t_sb = [held.tile([P, PIECE], F32, name=f"t{i}") for i in range(len(steps))]
        r_sb = [held.tile([P, PIECE], F32, name=f"r{i}") for i in range(len(steps))]
        cos_t = [held.tile([P, PIECE], F32, name=f"cos_t{i}") for i in range(len(steps))]
        sin_r = [held.tile([P, PIECE], F32, name=f"sin_r{i}") for i in range(len(steps))]

        def project(weights, i):
            piece = steps[i][0]
            product = psum.tile([P, PIECE], F32, name="product", tag="bank")
            for kb in range(KB):
                nc.tensor.matmul(
                    product[:],
                    weights[:, kb, :],
                    h_sb[:, kb, piece * PIECE : (piece + 1) * PIECE],
                    start=kb == 0,
                    stop=kb == KB - 1,
                )
            return product

        def make_t(i):
            cb = steps[i][1]
            nc.scalar.copy(t_sb[i][:], project(w_sb[:, :, cb * P : (cb + 1) * P], i)[:])

        def look_up_times(table, i, first, width, other, product):
            token = steps[i][0] * PIECE + first
            picked = offsets[:, token // 16 : (token + width) // 16]
            columns = slice(first, first + width)
            nc.vector.tensor_tensor(product[:, columns], table[:].indirect(picked), other[:, columns], MULT)

        totals = {}

        def open_sums(i):
            for first in (0, HALF):
                total = psum.tile([P, HALF], F32, name="total", tag="bank")
                nc.tensor.matmul(total[:], home[:], cos_t[i][:, first : first + HALF], start=True, stop=False)
                totals[i, first] = total

        def close_sum(i, first, turned):
            total = totals[i, first]
            nc.tensor.matmul(total[:], swap[:], sin_r[i][:, first : first + HALF], start=False, stop=True)
            nc.scalar.copy(turned, total[:])

        def out_columns(i, first):
            piece, cb = steps[i]
            token = piece * PIECE + first
            return out[cb * P : (cb + 1) * P, token : token + HALF]

        last = len(steps) - 1
        for i in range(last):
            make_t(i)
            nc.scalar.activation(r_sb[i][:], t_sb[i][:], IDENTITY, scale=sign[:])
            look_up_times(cos, i, 0, PIECE, t_sb[i], cos_t[i])
        last_r_ps = project(w_rot[:], last)
        for i in range(last - 1):
            open_sums(i)

        make_t(last)
        nc.scalar.copy(r_sb[last][:], last_r_ps[:])
        for i in range(last):
            look_up_times(sin_crossed, i, 0, PIECE, r_sb[i], sin_r[i])
        open_sums(last - 1)
        for i, first in [(i, first) for i in range(last) for first in (0, HALF)]:
            turned = sums.tile([P, HALF], F32, name="turned")
            close_sum(i, first, turned[:])
            nc.sync.dma_start(out_columns(i, first), turned[:])

        look_up_times(cos, last, 0, HALF, t_sb[last], cos_t[last])
        look_up_times(sin, last, 0, HALF, r_sb[last], sin_r[last])
        look_up_times(cos, last, HALF, HALF, t_sb[last], cos_t[last])

        def add_on_vector(first):
            columns = slice(first, first + HALF)
            turned = sums.tile([P, HALF], F32, name="turned")
            nc.vector.tensor_tensor(turned[:], cos_t[last][:, columns], sin_r[last][:, columns], ADD)
            nc.sync.dma_start(out_columns(last, first), turned[:])

        add_on_vector(0)
        look_up_times(sin, last, HALF, HALF, r_sb[last], sin_r[last])
        add_on_vector(HALF)
